import numpy as np
import ml_dtypes


def mxq(x, axis, fmt="e4m3"):
    dtype, down = {"e4m3": (ml_dtypes.float8_e4m3fn, 7), "e5m2": (ml_dtypes.float8_e5m2, 14)}[fmt]
    v = np.moveaxis(np.asarray(x, np.float32).astype(ml_dtypes.bfloat16).astype(np.float64), axis, -1)
    blocks = v.reshape(v.shape[:-1] + (-1, 32))
    amax = np.abs(blocks).max(-1, keepdims=True)
    byte = np.maximum(np.where(amax > 0, np.frexp(amax)[1] - 1 + 127, 0) - down, 1)
    scale = np.exp2(byte - 127.0)
    codes = (blocks / scale).astype(np.float32).astype(dtype).astype(np.float64)
    return np.moveaxis((codes * scale).reshape(v.shape), -1, axis)


WIDE = False


def mx_kscale(k):
    if not WIDE:
        return np.ones(k)
    levels = np.array([10, -10, 5, -5, 0])
    a = np.random.permutation(np.resize(levels, k // 512 * 4)).reshape(k // 512, 4)
    idx = np.arange(k)
    return np.exp2(a[idx // 512, idx % 128 // 32])


BF16 = ml_dtypes.bfloat16


def bf(x):
    return np.asarray(x, np.float32).astype(BF16)


def f64(x):
    return np.asarray(x).astype(np.float64)


B, N, IN_DIM, OUT_DIM, K = 4, 1024, 1024, 128, 3
EPS = 1e-6
SIG = 2.0


def laplacian(adj):
    d = adj.sum(axis=2)
    r = (d + EPS) ** -0.5
    return np.eye(N)[None] - r[:, :, None] * adj * r[:, None, :]


def setup_inputs():
    s = mx_kscale(N)
    return {"x": bf(np.random.standard_normal((B, N, IN_DIM)) * (s / s.max())[:, None]),
            "adj": bf(np.exp(SIG * np.random.standard_normal((B, N, N)) - SIG * SIG / 2.0) / N * (s * s)[:, None])}


def reference(x, adj):
    L = laplacian(f64(adj))
    return mxq(L, 2, "e4m3") @ mxq(f64(x), 1, "e4m3")

@@ -1,0 +1,226 @@
+from contextlib import ExitStack
+
+import concourse.mybir as mybir
+from concourse.masks import make_identity
+
+F32 = mybir.dt.float32
+BF16 = mybir.dt.bfloat16
+U32 = mybir.dt.uint32
+U8 = mybir.dt.uint8
+FP8X4 = mybir.dt.float8_e4m3fn_x4
+ALU = mybir.AluOpType
+ACT = mybir.ActivationFunctionType
+
+GRAPHS = 4
+NODES = 1024
+FEATURES = 1024
+EPS = 1e-6
+
+P = 128
+PACK = 4
+K_PASS = P * PACK
+PASSES = NODES // K_PASS
+PAIR = 2
+HALVES = PACK // PAIR
+ROW_BLOCKS = NODES // P
+GROUP = 2
+ROW_GROUPS = ROW_BLOCKS // GROUP
+SCALAR_SUMS = 6
+BANK = 512
+FEATURE_TILES = FEATURES // BANK
+
+FLOPS = 2 * GRAPHS * NODES * NODES * FEATURES
+
+
+def tile_cheblayer_pa_t_kernel(tc, x, adj, out):
+    nc = tc.nc
+    with ExitStack() as ctx:
+        const = ctx.enter_context(tc.tile_pool(name="const", bufs=1))
+        adj_pool = ctx.enter_context(tc.tile_pool(name="adj", bufs=GRAPHS))
+        x_pool = ctx.enter_context(tc.tile_pool(name="x", bufs=GRAPHS))
+        small = ctx.enter_context(tc.tile_pool(name="small", bufs=2))
+        unread = ctx.enter_context(tc.tile_pool(name="unread", bufs=2))
+        row_pool = ctx.enter_context(tc.tile_pool(name="r_row", bufs=2))
+        x_stage = ctx.enter_context(tc.tile_pool(name="x_stage", bufs=2))
+        x_mx = ctx.enter_context(tc.tile_pool(name="x_mx", bufs=2))
+        lap_stage = ctx.enter_context(tc.tile_pool(name="lap_stage", bufs=3))
+        lap_mx = ctx.enter_context(tc.tile_pool(name="lap_mx", bufs=3))
+        out_pool = ctx.enter_context(tc.tile_pool(name="out", bufs=3))
+        turn_psum = ctx.enter_context(tc.psum_pool(name="turn", bufs=4))
+        acc_psum = ctx.enter_context(tc.psum_pool(name="acc", bufs=4))
+
+        ident = const.tile([P, P], F32)
+        make_identity(nc, ident[:])
+
+        one = const.tile([P, 1], F32)
+        nc.vector.memset(one[:], 1.0)
+        warm = const.tile([P, 1], F32)
+        nc.scalar.sqrt(out=warm[:], in_=one[:])
+
+        def load_graph(g):
+            adj_sb = adj_pool.tile([P, ROW_BLOCKS, NODES], BF16)
+            for u in range(ROW_GROUPS):
+                blocks = slice(u * GROUP, (u + 1) * GROUP)
+                rows = slice(u * GROUP * P, (u + 1) * GROUP * P)
+                nc.sync.dma_start(
+                    out=adj_sb[:, blocks, :],
+                    in_=adj[g, rows, :].rearrange("(b p) j -> p b j", p=P),
+                )
+            x_sb = x_pool.tile([P, PASSES, PACK, FEATURES], BF16)
+            for s in range(PASSES):
+                rows = slice(s * K_PASS, (s + 1) * K_PASS)
+                nc.sync.dma_start(
+                    out=x_sb[:, s], in_=x[g, rows, :].rearrange("(p t) f -> p t f", t=PACK)
+                )
+            return adj_sb, x_sb
+
+        def degree_scales(adj_sb):
+            scalar_sums = small.tile([P, SCALAR_SUMS], F32)
+            for b in range(SCALAR_SUMS):
+                scalar_copy = unread.tile([P, NODES], BF16)
+                nc.scalar.activation(
+                    out=scalar_copy[:], in_=adj_sb[:, b, :], func=ACT.Copy,
+                    accum_out=scalar_sums[:, b : b + 1],
+                )
+            vector_sums = small.tile([P, ROW_BLOCKS - SCALAR_SUMS], F32)
+            for b in range(SCALAR_SUMS, ROW_BLOCKS):
+                vector_copy = unread.tile([P, NODES], BF16)
+                nc.vector.tensor_scalar(
+                    out=vector_copy[:], in0=adj_sb[:, b, :], scalar1=1.0, scalar2=None,
+                    op0=ALU.mult, op1=ALU.add,
+                    accum_out=vector_sums[:, b - SCALAR_SUMS : b - SCALAR_SUMS + 1],
+                )
+            shifted = small.tile([P, ROW_BLOCKS], F32)
+            nc.vector.tensor_scalar_add(
+                out=shifted[:, :SCALAR_SUMS], in0=scalar_sums[:], scalar1=EPS
+            )
+            nc.vector.tensor_scalar_add(
+                out=shifted[:, SCALAR_SUMS:], in0=vector_sums[:], scalar1=EPS
+            )
+            root = small.tile([P, ROW_BLOCKS], F32)
+            nc.scalar.sqrt(out=root[:], in_=shifted[:])
+            guess = small.tile([P, ROW_BLOCKS], F32)
+            nc.vector.reciprocal(out=guess[:], in_=root[:])
+            half_sq = small.tile([P, ROW_BLOCKS], F32)
+            nc.vector.scalar_tensor_tensor(
+                out=half_sq[:], in0=guess[:], scalar=0.5, in1=guess[:], op0=ALU.mult, op1=ALU.mult
+            )
+            near_half = small.tile([P, ROW_BLOCKS], F32)
+            nc.vector.tensor_mul(out=near_half[:], in0=half_sq[:], in1=shifted[:])
+            neg_r = small.tile([P, ROW_BLOCKS], F32)
+            nc.vector.scalar_tensor_tensor(
+                out=neg_r[:], in0=near_half[:], scalar=1.5, in1=guess[:],
+                op0=ALU.subtract, op1=ALU.mult,
+            )
+            r_row = row_pool.tile([P, NODES], F32)
+            blocks_per_bank = BANK // P
+            for h in range(NODES // BANK):
+                spread = turn_psum.tile([P, blocks_per_bank, P], F32, tag="turn")
+                for q in range(blocks_per_bank):
+                    b = h * blocks_per_bank + q
+                    nc.tensor.matmul(
+                        out=spread[:, q, :],
+                        lhsT=neg_r[:, b : b + 1].to_broadcast([P, P]),
+                        rhs=ident[:],
+                        start=True,
+                        stop=True,
+                    )
+                nc.scalar.mul(
+                    out=r_row[:, h * BANK : (h + 1) * BANK],
+                    in_=spread[:].rearrange("p q n -> p (q n)"),
+                    mul=-1.0,
+                )
+            return neg_r, r_row
+
+        def quantise_x(x_sb):
+            x_codes = x_mx.tile([P, PASSES, FEATURES], U32, align_bytes=64)
+            x_scales = x_mx.tile([P, PASSES, FEATURES], U8, align_bytes=64)
+            for s in range(PASSES):
+                grouped = x_stage.tile([P, FEATURES, PACK], BF16, align_bytes=64)
+                nc.vector.tensor_copy(
+                    out=grouped[:].rearrange("p (c i) t -> p c t i", i=4),
+                    in_=x_sb[:, s].rearrange("p t (c i) -> p c t i", i=4),
+                )
+                nc.vector.quantize_mx(
+                    out=x_codes[:, s, :].bitcast(FP8X4),
+                    scales=x_scales[:, s, :],
+                    in_=grouped[:].rearrange("p f t -> p (f t)"),
+                )
+            return x_codes, x_scales
+
+        def laplacian_rows(adj_sb, neg_r, r_row, b):
+            scale = neg_r[:, b : b + 1]
+            first, last = b * P, (b + 1) * P
+            for lo, hi in ((0, first), (last, NODES)):
+                if lo < hi:
+                    nc.vector.scalar_tensor_tensor(
+                        out=adj_sb[:, b, lo:hi], in0=adj_sb[:, b, lo:hi], scalar=scale,
+                        in1=r_row[:, lo:hi], op0=ALU.mult, op1=ALU.mult,
+                    )
+            product = small.tile([P, P], F32)
+            nc.vector.scalar_tensor_tensor(
+                out=product[:], in0=adj_sb[:, b, first:last], scalar=scale,
+                in1=r_row[:, first:last], op0=ALU.mult, op1=ALU.mult,
+            )
+            nc.vector.tensor_add(out=adj_sb[:, b, first:last], in0=product[:], in1=ident[:])
+
+        def quantise_rows(lap_sb, u):
+            words = lap_sb[:].bitcast(F32).rearrange(
+                "p b (s w h) -> p b s h w", s=PASSES, h=HALVES
+            )
+            grouped = lap_stage.tile([P, PASSES, GROUP, P, HALVES], F32, align_bytes=64)
+            for s in range(PASSES):
+                turned = turn_psum.tile([P, GROUP, HALVES, P], F32, tag="turn")
+                for b in range(GROUP):
+                    for h in range(HALVES):
+                        nc.tensor.transpose(
+                            turned[:, b, h, :], words[:, u * GROUP + b, s, h, :], ident[:]
+                        )
+                nc.scalar.copy(out=grouped[:, s], in_=turned[:].rearrange("p b h m -> p b m h"))
+            lap_codes = lap_mx.tile([P, PASSES * GROUP * P], U32, align_bytes=64)
+            lap_scales = lap_mx.tile([P, PASSES * GROUP * P], U8, align_bytes=64)
+            nc.vector.quantize_mx(
+                out=lap_codes[:].bitcast(FP8X4),
+                scales=lap_scales[:],
+                in_=grouped[:].rearrange("p s b m h -> p (s b m h)").bitcast(BF16),
+            )
+            return lap_codes, lap_scales
+
+        def multiply_and_store(g, u, lap_codes, lap_scales, x_codes, x_scales):
+            result = out_pool.tile([P, GROUP, FEATURES], F32)
+            for b in range(GROUP):
+                for n in range(FEATURE_TILES):
+                    cols = slice(n * BANK, (n + 1) * BANK)
+                    acc = acc_psum.tile([P, BANK], F32)
+                    for s in range(PASSES):
+                        rows = slice((s * GROUP + b) * P, (s * GROUP + b + 1) * P)
+                        nc.tensor.matmul_mx(
+                            out=acc[:],
+                            lhsT=lap_codes[:, rows].bitcast(FP8X4),
+                            lhsT_scale=lap_scales[:, rows],
+                            rhs=x_codes[:, s, cols].bitcast(FP8X4),
+                            rhs_scale=x_scales[:, s, cols],
+                            start=(s == 0),
+                            stop=(s == PASSES - 1),
+                        )
+                    nc.scalar.copy(out=result[:, b, cols], in_=acc[:])
+            rows = slice(u * GROUP * P, (u + 1) * GROUP * P)
+            nc.sync.dma_start(
+                out=out[g, rows, :].rearrange("(b p) f -> p b f", p=P), in_=result[:]
+            )
+
+        def prepare(adj_sb, x_sb):
+            return degree_scales(adj_sb) + quantise_x(x_sb)
+
+        inputs = [load_graph(g) for g in range(GRAPHS)]
+        prepared = prepare(*inputs[0])
+        for g in range(GRAPHS):
+            adj_sb = inputs[g][0]
+            neg_r, r_row, x_codes, x_scales = prepared
+            if g + 1 < GRAPHS:
+                prepared = prepare(*inputs[g + 1])
+            for u in range(ROW_GROUPS):
+                for b in range(u * GROUP, (u + 1) * GROUP):
+                    laplacian_rows(adj_sb, neg_r, r_row, b)
+                lap_codes, lap_scales = quantise_rows(adj_sb, u)
+                multiply_and_store(g, u, lap_codes, lap_scales, x_codes, x_scales)

@@ -25,11 +25,21 @@ HALVES = PACK // PAIR
 ROW_BLOCKS = NODES // P
 GROUP = 2
 ROW_GROUPS = ROW_BLOCKS // GROUP
-SCALAR_SUMS = 6
+STEPS = GRAPHS * ROW_GROUPS
 BANK = 512
 FEATURE_TILES = FEATURES // BANK
+X_WIDTH = PASSES * FEATURES // ROW_GROUPS
+
+LANE = 8
+SCALAR_SUMS = 6
+SUM_LEAD = ROW_GROUPS + 2
+X_LEAD = ROW_GROUPS - 1
 
 FLOPS = 2 * GRAPHS * NODES * NODES * FEATURES
+
+
+def sum_column(b):
+    return b if b < SCALAR_SUMS else LANE + b - SCALAR_SUMS
 
 
 def tile_cheblayer_pa_t_kernel(tc, x, adj, out):
@@ -38,9 +48,11 @@ def tile_cheblayer_pa_t_kernel(tc, x, adj, out):
         const = ctx.enter_context(tc.tile_pool(name="const", bufs=1))
         adj_pool = ctx.enter_context(tc.tile_pool(name="adj", bufs=GRAPHS))
         x_pool = ctx.enter_context(tc.tile_pool(name="x", bufs=GRAPHS))
+        sum_pool = ctx.enter_context(tc.tile_pool(name="sums", bufs=GRAPHS))
         small = ctx.enter_context(tc.tile_pool(name="small", bufs=2))
         unread = ctx.enter_context(tc.tile_pool(name="unread", bufs=2))
         row_pool = ctx.enter_context(tc.tile_pool(name="r_row", bufs=2))
+        diag_pool = ctx.enter_context(tc.tile_pool(name="diag", bufs=2 * GROUP))
         x_stage = ctx.enter_context(tc.tile_pool(name="x_stage", bufs=2))
         x_mx = ctx.enter_context(tc.tile_pool(name="x_mx", bufs=2))
         lap_stage = ctx.enter_context(tc.tile_pool(name="lap_stage", bufs=3))
@@ -51,63 +63,67 @@ def tile_cheblayer_pa_t_kernel(tc, x, adj, out):
 
         ident = const.tile([P, P], F32)
         make_identity(nc, ident[:])
+        eps = const.tile([P, 1], F32)
+        nc.vector.memset(eps[:], EPS)
 
-        one = const.tile([P, 1], F32)
-        nc.vector.memset(one[:], 1.0)
         warm = const.tile([P, 1], F32)
-        nc.scalar.sqrt(out=warm[:], in_=one[:])
+        nc.scalar.activation(out=warm[:], in_=eps[:], func=ACT.Abs_reciprocal_sqrt)
 
-        def load_graph(g):
+        adj_of, x_of, sums_of = [], [], []
+        for g in range(GRAPHS):
             adj_sb = adj_pool.tile([P, ROW_BLOCKS, NODES], BF16)
             for u in range(ROW_GROUPS):
-                blocks = slice(u * GROUP, (u + 1) * GROUP)
-                rows = slice(u * GROUP * P, (u + 1) * GROUP * P)
                 nc.sync.dma_start(
-                    out=adj_sb[:, blocks, :],
-                    in_=adj[g, rows, :].rearrange("(b p) j -> p b j", p=P),
+                    out=adj_sb[:, u * GROUP : (u + 1) * GROUP, :],
+                    in_=adj[g, u * GROUP * P : (u + 1) * GROUP * P, :].rearrange(
+                        "(b p) j -> p b j", p=P
+                    ),
                 )
             x_sb = x_pool.tile([P, PASSES, PACK, FEATURES], BF16)
             for s in range(PASSES):
-                rows = slice(s * K_PASS, (s + 1) * K_PASS)
                 nc.sync.dma_start(
-                    out=x_sb[:, s], in_=x[g, rows, :].rearrange("(p t) f -> p t f", t=PACK)
+                    out=x_sb[:, s],
+                    in_=x[g, s * K_PASS : (s + 1) * K_PASS, :].rearrange("(p t) f -> p t f", t=PACK),
                 )
-            return adj_sb, x_sb
+            sums = sum_pool.tile([P, 2 * LANE], F32)
+            nc.vector.memset(sums[:], 1.0)
+            adj_of.append(adj_sb)
+            x_of.append(x_sb)
+            sums_of.append(sums)
 
-        def degree_scales(adj_sb):
-            scalar_sums = small.tile([P, SCALAR_SUMS], F32)
-            for b in range(SCALAR_SUMS):
-                scalar_copy = unread.tile([P, NODES], BF16)
-                nc.scalar.activation(
-                    out=scalar_copy[:], in_=adj_sb[:, b, :], func=ACT.Copy,
-                    accum_out=scalar_sums[:, b : b + 1],
-                )
-            vector_sums = small.tile([P, ROW_BLOCKS - SCALAR_SUMS], F32)
-            for b in range(SCALAR_SUMS, ROW_BLOCKS):
-                vector_copy = unread.tile([P, NODES], BF16)
-                nc.vector.tensor_scalar(
-                    out=vector_copy[:], in0=adj_sb[:, b, :], scalar1=1.0, scalar2=None,
-                    op0=ALU.mult, op1=ALU.add,
-                    accum_out=vector_sums[:, b - SCALAR_SUMS : b - SCALAR_SUMS + 1],
-                )
-            shifted = small.tile([P, ROW_BLOCKS], F32)
-            nc.vector.tensor_scalar_add(
-                out=shifted[:, :SCALAR_SUMS], in0=scalar_sums[:], scalar1=EPS
+        def sum_rows(g, u):
+            for b in range(u * GROUP, (u + 1) * GROUP):
+                total = sums_of[g][:, sum_column(b) : sum_column(b) + 1]
+                if b < SCALAR_SUMS:
+                    scalar_copy = unread.tile([P, NODES], BF16)
+                    nc.scalar.activation(
+                        out=scalar_copy[:], in_=adj_of[g][:, b, :], func=ACT.Copy, accum_out=total
+                    )
+                else:
+                    vector_copy = unread.tile([P, NODES], BF16)
+                    nc.vector.tensor_scalar(
+                        out=vector_copy[:], in0=adj_of[g][:, b, :], scalar1=1.0, scalar2=None,
+                        op0=ALU.mult, op1=ALU.add, accum_out=total,
+                    )
+
+        def guess_scales(g):
+            guess = small.tile([P, 2 * LANE], F32)
+            nc.scalar.activation(
+                out=guess[:], in_=sums_of[g][:], func=ACT.Abs_reciprocal_sqrt, bias=eps[:]
             )
-            nc.vector.tensor_scalar_add(
-                out=shifted[:, SCALAR_SUMS:], in0=vector_sums[:], scalar1=EPS
-            )
-            root = small.tile([P, ROW_BLOCKS], F32)
-            nc.scalar.sqrt(out=root[:], in_=shifted[:])
-            guess = small.tile([P, ROW_BLOCKS], F32)
-            nc.vector.reciprocal(out=guess[:], in_=root[:])
-            half_sq = small.tile([P, ROW_BLOCKS], F32)
+            return guess
+
+        def refine_scales(g, guess):
+            half_sq = small.tile([P, 2 * LANE], F32)
             nc.vector.scalar_tensor_tensor(
                 out=half_sq[:], in0=guess[:], scalar=0.5, in1=guess[:], op0=ALU.mult, op1=ALU.mult
             )
-            near_half = small.tile([P, ROW_BLOCKS], F32)
-            nc.vector.tensor_mul(out=near_half[:], in0=half_sq[:], in1=shifted[:])
-            neg_r = small.tile([P, ROW_BLOCKS], F32)
+            near_half = small.tile([P, 2 * LANE], F32)
+            nc.vector.scalar_tensor_tensor(
+                out=near_half[:], in0=sums_of[g][:], scalar=EPS, in1=half_sq[:],
+                op0=ALU.add, op1=ALU.mult,
+            )
+            neg_r = small.tile([P, 2 * LANE], F32)
             nc.vector.scalar_tensor_tensor(
                 out=neg_r[:], in0=near_half[:], scalar=1.5, in1=guess[:],
                 op0=ALU.subtract, op1=ALU.mult,
@@ -117,10 +133,10 @@ def tile_cheblayer_pa_t_kernel(tc, x, adj, out):
             for h in range(NODES // BANK):
                 spread = turn_psum.tile([P, blocks_per_bank, P], F32, tag="turn")
                 for q in range(blocks_per_bank):
-                    b = h * blocks_per_bank + q
+                    column = sum_column(h * blocks_per_bank + q)
                     nc.tensor.matmul(
                         out=spread[:, q, :],
-                        lhsT=neg_r[:, b : b + 1].to_broadcast([P, P]),
+                        lhsT=neg_r[:, column : column + 1].to_broadcast([P, P]),
                         rhs=ident[:],
                         start=True,
                         stop=True,
@@ -132,57 +148,72 @@ def tile_cheblayer_pa_t_kernel(tc, x, adj, out):
                 )
             return neg_r, r_row
 
-        def quantise_x(x_sb):
-            x_codes = x_mx.tile([P, PASSES, FEATURES], U32, align_bytes=64)
-            x_scales = x_mx.tile([P, PASSES, FEATURES], U8, align_bytes=64)
-            for s in range(PASSES):
-                grouped = x_stage.tile([P, FEATURES, PACK], BF16, align_bytes=64)
-                nc.vector.tensor_copy(
-                    out=grouped[:].rearrange("p (c i) t -> p c t i", i=4),
-                    in_=x_sb[:, s].rearrange("p t (c i) -> p c t i", i=4),
-                )
-                nc.vector.quantize_mx(
-                    out=x_codes[:, s, :].bitcast(FP8X4),
-                    scales=x_scales[:, s, :],
-                    in_=grouped[:].rearrange("p f t -> p (f t)"),
-                )
-            return x_codes, x_scales
-
-        def laplacian_rows(adj_sb, neg_r, r_row, b):
-            scale = neg_r[:, b : b + 1]
-            first, last = b * P, (b + 1) * P
-            for lo, hi in ((0, first), (last, NODES)):
-                if lo < hi:
-                    nc.vector.scalar_tensor_tensor(
-                        out=adj_sb[:, b, lo:hi], in0=adj_sb[:, b, lo:hi], scalar=scale,
-                        in1=r_row[:, lo:hi], op0=ALU.mult, op1=ALU.mult,
-                    )
-            product = small.tile([P, P], F32)
-            nc.vector.scalar_tensor_tensor(
-                out=product[:], in0=adj_sb[:, b, first:last], scalar=scale,
-                in1=r_row[:, first:last], op0=ALU.mult, op1=ALU.mult,
+        def regroup_x(g, q):
+            s, n = divmod(q, ROW_GROUPS // PASSES)
+            grouped = x_stage.tile([P, X_WIDTH, PACK], BF16, align_bytes=64)
+            nc.vector.tensor_copy(
+                out=grouped[:].rearrange("p (c i) t -> p c t i", i=4),
+                in_=x_of[g][:, s, :, n * X_WIDTH : (n + 1) * X_WIDTH].rearrange(
+                    "p t (c i) -> p c t i", i=4
+                ),
             )
-            nc.vector.tensor_add(out=adj_sb[:, b, first:last], in0=product[:], in1=ident[:])
+            return grouped
 
-        def quantise_rows(lap_sb, u):
-            words = lap_sb[:].bitcast(F32).rearrange(
+        def quantise_x(q, grouped, x_codes, x_scales):
+            s, n = divmod(q, ROW_GROUPS // PASSES)
+            cols = slice(n * X_WIDTH, (n + 1) * X_WIDTH)
+            nc.vector.quantize_mx(
+                out=x_codes[:, s, cols].bitcast(FP8X4),
+                scales=x_scales[:, s, cols],
+                in_=grouped[:].rearrange("p f t -> p (f t)"),
+            )
+
+        def form_rows(g, u, neg_r, r_row):
+            adj_sb = adj_of[g]
+            blocks = range(u * GROUP, (u + 1) * GROUP)
+            products = {}
+            for b in blocks:
+                product = diag_pool.tile([P, P], F32)
+                nc.vector.scalar_tensor_tensor(
+                    out=product[:], in0=adj_sb[:, b, b * P : (b + 1) * P],
+                    scalar=neg_r[:, sum_column(b) : sum_column(b) + 1],
+                    in1=r_row[:, b * P : (b + 1) * P], op0=ALU.mult, op1=ALU.mult,
+                )
+                products[b] = product
+            for b in blocks:
+                for lo, hi in ((0, b * P), ((b + 1) * P, NODES)):
+                    if lo < hi:
+                        nc.vector.scalar_tensor_tensor(
+                            out=adj_sb[:, b, lo:hi], in0=adj_sb[:, b, lo:hi],
+                            scalar=neg_r[:, sum_column(b) : sum_column(b) + 1],
+                            in1=r_row[:, lo:hi], op0=ALU.mult, op1=ALU.mult,
+                        )
+                nc.vector.tensor_add(
+                    out=adj_sb[:, b, b * P : (b + 1) * P], in0=products[b][:], in1=ident[:]
+                )
+
+        def turn_rows(g, u):
+            words = adj_of[g][:].bitcast(F32).rearrange(
                 "p b (s w h) -> p b s h w", s=PASSES, h=HALVES
             )
-            grouped = lap_stage.tile([P, PASSES, GROUP, P, HALVES], F32, align_bytes=64)
-            for s in range(PASSES):
-                turned = turn_psum.tile([P, GROUP, HALVES, P], F32, tag="turn")
-                for b in range(GROUP):
+            grouped = lap_stage.tile([P, GROUP, PASSES, P, HALVES], F32, align_bytes=64)
+            for b in range(GROUP):
+                turned = turn_psum.tile([P, PASSES, HALVES, P], F32, tag="turn")
+                for s in range(PASSES):
                     for h in range(HALVES):
                         nc.tensor.transpose(
-                            turned[:, b, h, :], words[:, u * GROUP + b, s, h, :], ident[:]
+                            turned[:, s, h, :], words[:, u * GROUP + b, s, h, :], ident[:]
                         )
-                nc.scalar.copy(out=grouped[:, s], in_=turned[:].rearrange("p b h m -> p b m h"))
-            lap_codes = lap_mx.tile([P, PASSES * GROUP * P], U32, align_bytes=64)
-            lap_scales = lap_mx.tile([P, PASSES * GROUP * P], U8, align_bytes=64)
+                nc.scalar.copy(out=grouped[:, b], in_=turned[:].rearrange("p s h m -> p s m h"))
+            return grouped
+
+        def quantise_rows(grouped):
+            lap_codes = lap_mx.tile([P, GROUP * PASSES * P], U32, align_bytes=64)
+            lap_scales = lap_mx.tile([P, GROUP * PASSES * P], U8, align_bytes=64)
             nc.vector.quantize_mx(
                 out=lap_codes[:].bitcast(FP8X4),
                 scales=lap_scales[:],
-                in_=grouped[:].rearrange("p s b m h -> p (s b m h)").bitcast(BF16),
+                in_=grouped[:].rearrange("p b s m h -> p (b s m h)").bitcast(BF16),
             )
             return lap_codes, lap_scales
 
@@ -193,7 +224,7 @@ def tile_cheblayer_pa_t_kernel(tc, x, adj, out):
                     cols = slice(n * BANK, (n + 1) * BANK)
                     acc = acc_psum.tile([P, BANK], F32)
                     for s in range(PASSES):
-                        rows = slice((s * GROUP + b) * P, (s * GROUP + b + 1) * P)
+                        rows = slice((b * PASSES + s) * P, (b * PASSES + s + 1) * P)
                         nc.tensor.matmul_mx(
                             out=acc[:],
                             lhsT=lap_codes[:, rows].bitcast(FP8X4),
@@ -204,23 +235,41 @@ def tile_cheblayer_pa_t_kernel(tc, x, adj, out):
                             stop=(s == PASSES - 1),
                         )
                     nc.scalar.copy(out=result[:, b, cols], in_=acc[:])
-            rows = slice(u * GROUP * P, (u + 1) * GROUP * P)
             nc.sync.dma_start(
-                out=out[g, rows, :].rearrange("(b p) f -> p b f", p=P), in_=result[:]
+                out=out[g, u * GROUP * P : (u + 1) * GROUP * P, :].rearrange(
+                    "(b p) f -> p b f", p=P
+                ),
+                in_=result[:],
             )
 
-        def prepare(adj_sb, x_sb):
-            return degree_scales(adj_sb) + quantise_x(x_sb)
+        guess_of, scales_of, x_mx_of = {}, {}, {}
+        grouped_of = {}
+        for step in range(-SUM_LEAD, STEPS + 1):
+            g, u = divmod(step + SUM_LEAD, ROW_GROUPS)
+            if g < GRAPHS:
+                sum_rows(g, u)
+                if u == ROW_GROUPS - 1:
+                    guess_of[g] = guess_scales(g)
+            if u == 0 and 0 < g <= GRAPHS:
+                scales_of[g - 1] = refine_scales(g - 1, guess_of[g - 1])
 
-        inputs = [load_graph(g) for g in range(GRAPHS)]
-        prepared = prepare(*inputs[0])
-        for g in range(GRAPHS):
-            adj_sb = inputs[g][0]
-            neg_r, r_row, x_codes, x_scales = prepared
-            if g + 1 < GRAPHS:
-                prepared = prepare(*inputs[g + 1])
-            for u in range(ROW_GROUPS):
-                for b in range(u * GROUP, (u + 1) * GROUP):
-                    laplacian_rows(adj_sb, neg_r, r_row, b)
-                lap_codes, lap_scales = quantise_rows(adj_sb, u)
-                multiply_and_store(g, u, lap_codes, lap_scales, x_codes, x_scales)
+            x_g, x_q = divmod(step + X_LEAD, ROW_GROUPS)
+            x_due = 0 <= step + X_LEAD < STEPS
+            if x_due:
+                if x_q == 0:
+                    x_codes = x_mx.tile([P, PASSES, FEATURES], U32, align_bytes=64)
+                    x_scales = x_mx.tile([P, PASSES, FEATURES], U8, align_bytes=64)
+                    x_mx_of[x_g] = (x_codes, x_scales)
+                x_grouped = regroup_x(x_g, x_q)
+
+            if 0 <= step < STEPS:
+                g, u = divmod(step, ROW_GROUPS)
+                form_rows(g, u, *scales_of[g])
+                grouped_of[step] = turn_rows(g, u)
+            if 0 <= step - 1:
+                lap_codes, lap_scales = quantise_rows(grouped_of[step - 1])
+            if x_due:
+                quantise_x(x_q, x_grouped, *x_mx_of[x_g])
+            if 0 <= step - 1:
+                g, u = divmod(step - 1, ROW_GROUPS)
+                multiply_and_store(g, u, lap_codes, lap_scales, *x_mx_of[g])

@@ -23,7 +23,7 @@ PASSES = NODES // K_PASS
 PAIR = 2
 HALVES = PACK // PAIR
 ROW_BLOCKS = NODES // P
-GROUP = 2
+GROUP = 1
 ROW_GROUPS = ROW_BLOCKS // GROUP
 STEPS = GRAPHS * ROW_GROUPS
 BANK = 512
@@ -31,15 +31,19 @@ FEATURE_TILES = FEATURES // BANK
 X_WIDTH = PASSES * FEATURES // ROW_GROUPS
 
 LANE = 8
-SCALAR_SUMS = 6
-SUM_LEAD = ROW_GROUPS + 2
+IN_FLIGHT = 6
+SUM_LEAD = ROW_GROUPS + 4 // GROUP
 X_LEAD = ROW_GROUPS - 1
 
 FLOPS = 2 * GRAPHS * NODES * NODES * FEATURES
 
 
-def sum_column(b):
-    return b if b < SCALAR_SUMS else LANE + b - SCALAR_SUMS
+def scalar_sums(g):
+    return ROW_BLOCKS // 2 if g == 0 else ROW_BLOCKS - 1
+
+
+def sum_column(g, b):
+    return b if b < scalar_sums(g) else LANE + b - scalar_sums(g)
 
 
 def tile_cheblayer_pa_t_kernel(tc, x, adj, out):
@@ -52,12 +56,12 @@ def tile_cheblayer_pa_t_kernel(tc, x, adj, out):
         small = ctx.enter_context(tc.tile_pool(name="small", bufs=2))
         unread = ctx.enter_context(tc.tile_pool(name="unread", bufs=2))
         row_pool = ctx.enter_context(tc.tile_pool(name="r_row", bufs=2))
-        diag_pool = ctx.enter_context(tc.tile_pool(name="diag", bufs=2 * GROUP))
+        diag_pool = ctx.enter_context(tc.tile_pool(name="diag", bufs=4))
         x_stage = ctx.enter_context(tc.tile_pool(name="x_stage", bufs=2))
         x_mx = ctx.enter_context(tc.tile_pool(name="x_mx", bufs=2))
-        lap_stage = ctx.enter_context(tc.tile_pool(name="lap_stage", bufs=3))
-        lap_mx = ctx.enter_context(tc.tile_pool(name="lap_mx", bufs=3))
-        out_pool = ctx.enter_context(tc.tile_pool(name="out", bufs=3))
+        lap_stage = ctx.enter_context(tc.tile_pool(name="lap_stage", bufs=IN_FLIGHT // GROUP))
+        lap_mx = ctx.enter_context(tc.tile_pool(name="lap_mx", bufs=IN_FLIGHT // GROUP))
+        out_pool = ctx.enter_context(tc.tile_pool(name="out", bufs=IN_FLIGHT // GROUP))
         turn_psum = ctx.enter_context(tc.psum_pool(name="turn", bufs=4))
         acc_psum = ctx.enter_context(tc.psum_pool(name="acc", bufs=4))
 
@@ -93,8 +97,8 @@ def tile_cheblayer_pa_t_kernel(tc, x, adj, out):
 
         def sum_rows(g, u):
             for b in range(u * GROUP, (u + 1) * GROUP):
-                total = sums_of[g][:, sum_column(b) : sum_column(b) + 1]
-                if b < SCALAR_SUMS:
+                total = sums_of[g][:, sum_column(g, b) : sum_column(g, b) + 1]
+                if b < scalar_sums(g):
                     scalar_copy = unread.tile([P, NODES], BF16)
                     nc.scalar.activation(
                         out=scalar_copy[:], in_=adj_of[g][:, b, :], func=ACT.Copy, accum_out=total
@@ -133,7 +137,7 @@ def tile_cheblayer_pa_t_kernel(tc, x, adj, out):
             for h in range(NODES // BANK):
                 spread = turn_psum.tile([P, blocks_per_bank, P], F32, tag="turn")
                 for q in range(blocks_per_bank):
-                    column = sum_column(h * blocks_per_bank + q)
+                    column = sum_column(g, h * blocks_per_bank + q)
                     nc.tensor.matmul(
                         out=spread[:, q, :],
                         lhsT=neg_r[:, column : column + 1].to_broadcast([P, P]),
@@ -176,7 +180,7 @@ def tile_cheblayer_pa_t_kernel(tc, x, adj, out):
                 product = diag_pool.tile([P, P], F32)
                 nc.vector.scalar_tensor_tensor(
                     out=product[:], in0=adj_sb[:, b, b * P : (b + 1) * P],
-                    scalar=neg_r[:, sum_column(b) : sum_column(b) + 1],
+                    scalar=neg_r[:, sum_column(g, b) : sum_column(g, b) + 1],
                     in1=r_row[:, b * P : (b + 1) * P], op0=ALU.mult, op1=ALU.mult,
                 )
                 products[b] = product
@@ -185,7 +189,7 @@ def tile_cheblayer_pa_t_kernel(tc, x, adj, out):
                     if lo < hi:
                         nc.vector.scalar_tensor_tensor(
                             out=adj_sb[:, b, lo:hi], in0=adj_sb[:, b, lo:hi],
-                            scalar=neg_r[:, sum_column(b) : sum_column(b) + 1],
+                            scalar=neg_r[:, sum_column(g, b) : sum_column(g, b) + 1],
                             in1=r_row[:, lo:hi], op0=ALU.mult, op1=ALU.mult,
                         )
                 nc.vector.tensor_add(

@@ -23,7 +23,7 @@ PASSES = NODES // K_PASS
 PAIR = 2
 HALVES = PACK // PAIR
 ROW_BLOCKS = NODES // P
-GROUP = 1
+GROUP = 2
 ROW_GROUPS = ROW_BLOCKS // GROUP
 STEPS = GRAPHS * ROW_GROUPS
 BANK = 512
@@ -39,7 +39,7 @@ FLOPS = 2 * GRAPHS * NODES * NODES * FEATURES
 
 
 def scalar_sums(g):
-    return ROW_BLOCKS // 2 if g == 0 else ROW_BLOCKS - 1
+    return ROW_BLOCKS // 2 if g == 0 else ROW_BLOCKS - 2
 
 
 def sum_column(g, b):
@@ -61,7 +61,7 @@ def tile_cheblayer_pa_t_kernel(tc, x, adj, out):
         x_mx = ctx.enter_context(tc.tile_pool(name="x_mx", bufs=2))
         lap_stage = ctx.enter_context(tc.tile_pool(name="lap_stage", bufs=IN_FLIGHT // GROUP))
         lap_mx = ctx.enter_context(tc.tile_pool(name="lap_mx", bufs=IN_FLIGHT // GROUP))
-        out_pool = ctx.enter_context(tc.tile_pool(name="out", bufs=IN_FLIGHT // GROUP))
+        out_pool = ctx.enter_context(tc.tile_pool(name="out", bufs=IN_FLIGHT))
         turn_psum = ctx.enter_context(tc.psum_pool(name="turn", bufs=4))
         acc_psum = ctx.enter_context(tc.psum_pool(name="acc", bufs=4))
 
@@ -86,8 +86,10 @@ def tile_cheblayer_pa_t_kernel(tc, x, adj, out):
             x_sb = x_pool.tile([P, PASSES, PACK, FEATURES], BF16)
             for s in range(PASSES):
                 nc.sync.dma_start(
-                    out=x_sb[:, s],
-                    in_=x[g, s * K_PASS : (s + 1) * K_PASS, :].rearrange("(p t) f -> p t f", t=PACK),
+                    out=x_sb[:, s].rearrange("p (h e) f -> p h e f", h=HALVES),
+                    in_=x[g, s * K_PASS : (s + 1) * K_PASS, :].rearrange(
+                        "(h p e) f -> p h e f", h=HALVES, e=PAIR
+                    ),
                 )
             sums = sum_pool.tile([P, 2 * LANE], F32)
             nc.vector.memset(sums[:], 1.0)
@@ -198,7 +200,7 @@ def tile_cheblayer_pa_t_kernel(tc, x, adj, out):
 
         def turn_rows(g, u):
             words = adj_of[g][:].bitcast(F32).rearrange(
-                "p b (s w h) -> p b s h w", s=PASSES, h=HALVES
+                "p b (s h w) -> p b s h w", s=PASSES, h=HALVES
             )
             grouped = lap_stage.tile([P, GROUP, PASSES, P, HALVES], F32, align_bytes=64)
             for b in range(GROUP):
@@ -222,8 +224,8 @@ def tile_cheblayer_pa_t_kernel(tc, x, adj, out):
             return lap_codes, lap_scales
 
         def multiply_and_store(g, u, lap_codes, lap_scales, x_codes, x_scales):
-            result = out_pool.tile([P, GROUP, FEATURES], F32)
             for b in range(GROUP):
+                result = out_pool.tile([P, FEATURES], F32)
                 for n in range(FEATURE_TILES):
                     cols = slice(n * BANK, (n + 1) * BANK)
                     acc = acc_psum.tile([P, BANK], F32)
@@ -238,13 +240,9 @@ def tile_cheblayer_pa_t_kernel(tc, x, adj, out):
                             start=(s == 0),
                             stop=(s == PASSES - 1),
                         )
-                    nc.scalar.copy(out=result[:, b, cols], in_=acc[:])
-            nc.sync.dma_start(
-                out=out[g, u * GROUP * P : (u + 1) * GROUP * P, :].rearrange(
-                    "(b p) f -> p b f", p=P
-                ),
-                in_=result[:],
-            )
+                    nc.scalar.copy(out=result[:, cols], in_=acc[:])
+                first_row = (u * GROUP + b) * P
+                nc.sync.dma_start(out=out[g, first_row : first_row + P, :], in_=result[:])
 
         guess_of, scales_of, x_mx_of = {}, {}, {}
         grouped_of = {}

from contextlib import ExitStack

import concourse.mybir as mybir
from concourse.masks import make_identity

F32 = mybir.dt.float32
BF16 = mybir.dt.bfloat16
U32 = mybir.dt.uint32
U8 = mybir.dt.uint8
FP8X4 = mybir.dt.float8_e4m3fn_x4
ALU = mybir.AluOpType
ACT = mybir.ActivationFunctionType

GRAPHS = 4
NODES = 1024
FEATURES = 1024
EPS = 1e-6

P = 128
PACK = 4
K_PASS = P * PACK
PASSES = NODES // K_PASS
PAIR = 2
HALVES = PACK // PAIR
ROW_BLOCKS = NODES // P
GROUP = 2
ROW_GROUPS = ROW_BLOCKS // GROUP
STEPS = GRAPHS * ROW_GROUPS
BANK = 512
FEATURE_TILES = FEATURES // BANK
X_WIDTH = PASSES * FEATURES // ROW_GROUPS

LANE = 8
IN_FLIGHT = 6
SUM_LEAD = ROW_GROUPS + 4 // GROUP
X_LEAD = ROW_GROUPS - 1

FLOPS = 2 * GRAPHS * NODES * NODES * FEATURES


def scalar_sums(g):
    return ROW_BLOCKS // 2 if g == 0 else ROW_BLOCKS - 2


def sum_column(g, b):
    return b if b < scalar_sums(g) else LANE + b - scalar_sums(g)


def tile_cheblayer_pa_t_kernel(tc, x, adj, out):
    nc = tc.nc
    with ExitStack() as ctx:
        const = ctx.enter_context(tc.tile_pool(name="const", bufs=1))
        adj_pool = ctx.enter_context(tc.tile_pool(name="adj", bufs=GRAPHS))
        x_pool = ctx.enter_context(tc.tile_pool(name="x", bufs=GRAPHS))
        sum_pool = ctx.enter_context(tc.tile_pool(name="sums", bufs=GRAPHS))
        small = ctx.enter_context(tc.tile_pool(name="small", bufs=2))
        unread = ctx.enter_context(tc.tile_pool(name="unread", bufs=2))
        row_pool = ctx.enter_context(tc.tile_pool(name="r_row", bufs=2))
        diag_pool = ctx.enter_context(tc.tile_pool(name="diag", bufs=4))
        x_stage = ctx.enter_context(tc.tile_pool(name="x_stage", bufs=2))
        x_mx = ctx.enter_context(tc.tile_pool(name="x_mx", bufs=2))
        lap_stage = ctx.enter_context(tc.tile_pool(name="lap_stage", bufs=IN_FLIGHT // GROUP))
        lap_mx = ctx.enter_context(tc.tile_pool(name="lap_mx", bufs=IN_FLIGHT // GROUP))
        out_pool = ctx.enter_context(tc.tile_pool(name="out", bufs=IN_FLIGHT))
        turn_psum = ctx.enter_context(tc.psum_pool(name="turn", bufs=4))
        acc_psum = ctx.enter_context(tc.psum_pool(name="acc", bufs=4))

        ident = const.tile([P, P], F32)
        make_identity(nc, ident[:])
        eps = const.tile([P, 1], F32)
        nc.vector.memset(eps[:], EPS)

        warm = const.tile([P, 1], F32)
        nc.scalar.activation(out=warm[:], in_=eps[:], func=ACT.Abs_reciprocal_sqrt)

        adj_of, x_of, sums_of = [], [], []
        for g in range(GRAPHS):
            adj_sb = adj_pool.tile([P, ROW_BLOCKS, NODES], BF16)
            for u in range(ROW_GROUPS):
                nc.sync.dma_start(
                    out=adj_sb[:, u * GROUP : (u + 1) * GROUP, :],
                    in_=adj[g, u * GROUP * P : (u + 1) * GROUP * P, :].rearrange(
                        "(b p) j -> p b j", p=P
                    ),
                )
            x_sb = x_pool.tile([P, PASSES, PACK, FEATURES], BF16)
            for s in range(PASSES):
                nc.sync.dma_start(
                    out=x_sb[:, s].rearrange("p (h e) f -> p h e f", h=HALVES),
                    in_=x[g, s * K_PASS : (s + 1) * K_PASS, :].rearrange(
                        "(h p e) f -> p h e f", h=HALVES, e=PAIR
                    ),
                )
            sums = sum_pool.tile([P, 2 * LANE], F32)
            nc.vector.memset(sums[:], 1.0)
            adj_of.append(adj_sb)
            x_of.append(x_sb)
            sums_of.append(sums)

        def sum_rows(g, u):
            for b in range(u * GROUP, (u + 1) * GROUP):
                total = sums_of[g][:, sum_column(g, b) : sum_column(g, b) + 1]
                if b < scalar_sums(g):
                    scalar_copy = unread.tile([P, NODES], BF16)
                    nc.scalar.activation(
                        out=scalar_copy[:], in_=adj_of[g][:, b, :], func=ACT.Copy, accum_out=total
                    )
                else:
                    vector_copy = unread.tile([P, NODES], BF16)
                    nc.vector.tensor_scalar(
                        out=vector_copy[:], in0=adj_of[g][:, b, :], scalar1=1.0, scalar2=None,
                        op0=ALU.mult, op1=ALU.add, accum_out=total,
                    )

        def guess_scales(g):
            guess = small.tile([P, 2 * LANE], F32)
            nc.scalar.activation(
                out=guess[:], in_=sums_of[g][:], func=ACT.Abs_reciprocal_sqrt, bias=eps[:]
            )
            return guess

        def refine_scales(g, guess):
            half_sq = small.tile([P, 2 * LANE], F32)
            nc.vector.scalar_tensor_tensor(
                out=half_sq[:], in0=guess[:], scalar=0.5, in1=guess[:], op0=ALU.mult, op1=ALU.mult
            )
            near_half = small.tile([P, 2 * LANE], F32)
            nc.vector.scalar_tensor_tensor(
                out=near_half[:], in0=sums_of[g][:], scalar=EPS, in1=half_sq[:],
                op0=ALU.add, op1=ALU.mult,
            )
            neg_r = small.tile([P, 2 * LANE], F32)
            nc.vector.scalar_tensor_tensor(
                out=neg_r[:], in0=near_half[:], scalar=1.5, in1=guess[:],
                op0=ALU.subtract, op1=ALU.mult,
            )
            r_row = row_pool.tile([P, NODES], F32)
            blocks_per_bank = BANK // P
            for h in range(NODES // BANK):
                spread = turn_psum.tile([P, blocks_per_bank, P], F32, tag="turn")
                for q in range(blocks_per_bank):
                    column = sum_column(g, h * blocks_per_bank + q)
                    nc.tensor.matmul(
                        out=spread[:, q, :],
                        lhsT=neg_r[:, column : column + 1].to_broadcast([P, P]),
                        rhs=ident[:],
                        start=True,
                        stop=True,
                    )
                nc.scalar.mul(
                    out=r_row[:, h * BANK : (h + 1) * BANK],
                    in_=spread[:].rearrange("p q n -> p (q n)"),
                    mul=-1.0,
                )
            return neg_r, r_row

        def regroup_x(g, q):
            s, n = divmod(q, ROW_GROUPS // PASSES)
            grouped = x_stage.tile([P, X_WIDTH, PACK], BF16, align_bytes=64)
            nc.vector.tensor_copy(
                out=grouped[:].rearrange("p (c i) t -> p c t i", i=4),
                in_=x_of[g][:, s, :, n * X_WIDTH : (n + 1) * X_WIDTH].rearrange(
                    "p t (c i) -> p c t i", i=4
                ),
            )
            return grouped

        def quantise_x(q, grouped, x_codes, x_scales):
            s, n = divmod(q, ROW_GROUPS // PASSES)
            cols = slice(n * X_WIDTH, (n + 1) * X_WIDTH)
            nc.vector.quantize_mx(
                out=x_codes[:, s, cols].bitcast(FP8X4),
                scales=x_scales[:, s, cols],
                in_=grouped[:].rearrange("p f t -> p (f t)"),
            )

        def form_rows(g, u, neg_r, r_row):
            adj_sb = adj_of[g]
            blocks = range(u * GROUP, (u + 1) * GROUP)
            products = {}
            for b in blocks:
                product = diag_pool.tile([P, P], F32)
                nc.vector.scalar_tensor_tensor(
                    out=product[:], in0=adj_sb[:, b, b * P : (b + 1) * P],
                    scalar=neg_r[:, sum_column(g, b) : sum_column(g, b) + 1],
                    in1=r_row[:, b * P : (b + 1) * P], op0=ALU.mult, op1=ALU.mult,
                )
                products[b] = product
            for b in blocks:
                for lo, hi in ((0, b * P), ((b + 1) * P, NODES)):
                    if lo < hi:
                        nc.vector.scalar_tensor_tensor(
                            out=adj_sb[:, b, lo:hi], in0=adj_sb[:, b, lo:hi],
                            scalar=neg_r[:, sum_column(g, b) : sum_column(g, b) + 1],
                            in1=r_row[:, lo:hi], op0=ALU.mult, op1=ALU.mult,
                        )
                nc.vector.tensor_add(
                    out=adj_sb[:, b, b * P : (b + 1) * P], in0=products[b][:], in1=ident[:]
                )

        def turn_rows(g, u):
            words = adj_of[g][:].bitcast(F32).rearrange(
                "p b (s h w) -> p b s h w", s=PASSES, h=HALVES
            )
            grouped = lap_stage.tile([P, GROUP, PASSES, P, HALVES], F32, align_bytes=64)
            for b in range(GROUP):
                turned = turn_psum.tile([P, PASSES, HALVES, P], F32, tag="turn")
                for s in range(PASSES):
                    for h in range(HALVES):
                        nc.tensor.transpose(
                            turned[:, s, h, :], words[:, u * GROUP + b, s, h, :], ident[:]
                        )
                nc.scalar.copy(out=grouped[:, b], in_=turned[:].rearrange("p s h m -> p s m h"))
            return grouped

        def quantise_rows(grouped):
            lap_codes = lap_mx.tile([P, GROUP * PASSES * P], U32, align_bytes=64)
            lap_scales = lap_mx.tile([P, GROUP * PASSES * P], U8, align_bytes=64)
            nc.vector.quantize_mx(
                out=lap_codes[:].bitcast(FP8X4),
                scales=lap_scales[:],
                in_=grouped[:].rearrange("p b s m h -> p (b s m h)").bitcast(BF16),
            )
            return lap_codes, lap_scales

        def multiply_and_store(g, u, lap_codes, lap_scales, x_codes, x_scales):
            for b in range(GROUP):
                result = out_pool.tile([P, FEATURES], F32)
                for n in range(FEATURE_TILES):
                    cols = slice(n * BANK, (n + 1) * BANK)
                    acc = acc_psum.tile([P, BANK], F32)
                    for s in range(PASSES):
                        rows = slice((b * PASSES + s) * P, (b * PASSES + s + 1) * P)
                        nc.tensor.matmul_mx(
                            out=acc[:],
                            lhsT=lap_codes[:, rows].bitcast(FP8X4),
                            lhsT_scale=lap_scales[:, rows],
                            rhs=x_codes[:, s, cols].bitcast(FP8X4),
                            rhs_scale=x_scales[:, s, cols],
                            start=(s == 0),
                            stop=(s == PASSES - 1),
                        )
                    nc.scalar.copy(out=result[:, cols], in_=acc[:])
                first_row = (u * GROUP + b) * P
                nc.sync.dma_start(out=out[g, first_row : first_row + P, :], in_=result[:])

        guess_of, scales_of, x_mx_of = {}, {}, {}
        grouped_of = {}
        for step in range(-SUM_LEAD, STEPS + 1):
            g, u = divmod(step + SUM_LEAD, ROW_GROUPS)
            if g < GRAPHS:
                sum_rows(g, u)
                if u == ROW_GROUPS - 1:
                    guess_of[g] = guess_scales(g)
            if u == 0 and 0 < g <= GRAPHS:
                scales_of[g - 1] = refine_scales(g - 1, guess_of[g - 1])

            x_g, x_q = divmod(step + X_LEAD, ROW_GROUPS)
            x_due = 0 <= step + X_LEAD < STEPS
            if x_due:
                if x_q == 0:
                    x_codes = x_mx.tile([P, PASSES, FEATURES], U32, align_bytes=64)
                    x_scales = x_mx.tile([P, PASSES, FEATURES], U8, align_bytes=64)
                    x_mx_of[x_g] = (x_codes, x_scales)
                x_grouped = regroup_x(x_g, x_q)

            if 0 <= step < STEPS:
                g, u = divmod(step, ROW_GROUPS)
                form_rows(g, u, *scales_of[g])
                grouped_of[step] = turn_rows(g, u)
            if 0 <= step - 1:
                lap_codes, lap_scales = quantise_rows(grouped_of[step - 1])
            if x_due:
                quantise_x(x_q, x_grouped, *x_mx_of[x_g])
            if 0 <= step - 1:
                g, u = divmod(step - 1, ROW_GROUPS)
                multiply_and_store(g, u, lap_codes, lap_scales, *x_mx_of[g])
